import numpy as np
import ml_dtypes


def mxq(x, axis, fmt="e4m3"):
    dtype, down = {"e4m3": (ml_dtypes.float8_e4m3fn, 7), "e5m2": (ml_dtypes.float8_e5m2, 14)}[fmt]
    v = np.moveaxis(np.asarray(x, np.float32).astype(ml_dtypes.bfloat16).astype(np.float64), axis, -1)
    blocks = v.reshape(v.shape[:-1] + (-1, 32))
    amax = np.abs(blocks).max(-1, keepdims=True)
    byte = np.maximum(np.where(amax > 0, np.frexp(amax)[1] - 1 + 127, 0) - down, 1)
    scale = np.exp2(byte - 127.0)
    codes = (blocks / scale).astype(np.float32).astype(dtype).astype(np.float64)
    return np.moveaxis((codes * scale).reshape(v.shape), -1, axis)


WIDE = False


def mx_kscale(k):
    if not WIDE:
        return np.ones(k)
    levels = np.array([10, -10, 5, -5, 0])
    a = np.random.permutation(np.resize(levels, k // 512 * 4)).reshape(k // 512, 4)
    idx = np.arange(k)
    return np.exp2(a[idx // 512, idx % 128 // 32])


BF16 = ml_dtypes.bfloat16


def bf(x):
    return np.asarray(x, np.float32).astype(BF16)


def f64(x):
    return np.asarray(x).astype(np.float64)


B, T, C, A, H = 4, 256, 1024, 1024, 16


def sigmoid(v):
    return 1.0 / (1.0 + np.exp(-v))


def setup_inputs():
    s, t = mx_kscale(C), mx_kscale(A)
    return {"x": bf(np.random.standard_normal((B, T, C)) * s),
            "time_mix": bf(np.random.uniform(0.0, 1.0, (1, 1, C))),
            "Wr": bf(np.random.standard_normal((A, C)) * 1.5 / np.sqrt(C) / s[None, :]),
            "wkv": bf(np.random.standard_normal((B, T, A)) * 1.3 * t),
            "sum_k": bf(np.exp(1.0 + 0.6 * np.random.standard_normal((B, T, A)))),
            "Wo": bf(np.random.standard_normal((C, A)) * 1.5 / np.sqrt(A) / t[None, :])}


def reference(x, time_mix, Wr, wkv, sum_k, Wo):
    x, tm = f64(x), f64(time_mix)
    xs = np.concatenate([np.zeros_like(x[:, :1]), x[:, :-1]], axis=1)
    xm = x * tm + xs * (1.0 - tm)
    r = mxq(xm, 2, "e4m3") @ mxq(f64(Wr), 1, "e4m3").T
    g = sigmoid(r) * f64(wkv) / f64(sum_k)
    return mxq(g, 2, "e4m3") @ mxq(f64(Wo), 1, "e4m3").T

@@ -1,0 +1,270 @@
+import concourse.mybir as mybir
+from concourse.masks import make_identity
+
+F32 = mybir.dt.float32
+BF16 = mybir.dt.bfloat16
+U32 = mybir.dt.uint32
+U8 = mybir.dt.uint8
+FP8X4 = mybir.dt.float8_e4m3fn_x4
+ACT = mybir.ActivationFunctionType
+ALU = mybir.AluOpType
+
+P = 128
+TOKENS = 1024
+SEQ = 256
+CH = 1024
+PASSES = 2
+BLOCKS = 4
+HALF = 512
+N_TILES = TOKENS // P
+PAD = 8
+
+FLOPS = 2 * 2 * TOKENS * CH * CH
+
+
+def tile_rwkv2timemix_pa_kernel(tc, x, time_mix, Wr, wkv, sum_k, Wo, out):
+    nc = tc.nc
+    x_rows = x.flatten_outer_dims()
+    wkv_rows = wkv.flatten_outer_dims()
+    sum_k_rows = sum_k.flatten_outer_dims()
+    out_rows = out.flatten_outer_dims()
+
+    with tc.tile_pool(name="consts", bufs=1) as consts, tc.tile_pool(
+        name="inputs", bufs=4
+    ) as inputs, tc.tile_pool(name="keep", bufs=1) as keep, tc.tile_pool(
+        name="work", bufs=4
+    ) as work, tc.psum_pool(name="psum", bufs=8) as psum, tc.manual_schedule():
+        ident = consts.tile([P, P], F32, name="ident")
+        make_identity(nc, ident[:])
+        tm_pairs = consts.tile([P, BLOCKS, 2], BF16, name="tm_pairs")
+        nc.scalar.dma_start(
+            out=tm_pairs[:], in_=time_mix.squeeze().rearrange("(h p e) -> p h e", p=P, e=2)
+        )
+        tm_col = consts.tile([P, 2 * BLOCKS], F32, name="tm_col")
+        nc.vector.tensor_copy(out=tm_col[:], in_=tm_pairs[:].rearrange("p h e -> p (h e)"))
+        rest_col = consts.tile([P, 2 * BLOCKS], F32, name="rest_col")
+        nc.vector.tensor_scalar(
+            out=rest_col[:], in0=tm_col[:], scalar1=-1.0, scalar2=1.0, op0=ALU.mult, op1=ALU.add
+        )
+
+        def load_pair(rows, n, name):
+            pair = inputs.tile([P, 2, CH], BF16, name=name + str(n), tag=name)
+            nc.sync.dma_start(
+                out=pair[:], in_=rows[2 * P * n : 2 * P * (n + 1), :].rearrange("(i p) c -> p i c", p=P)
+            )
+            return pair
+
+        def load_wr(j):
+            pair = inputs.tile([P, 2, CH], BF16, name="wr" + str(j), tag="wr")
+            nc.sync.dma_start(
+                out=pair[:], in_=Wr[2 * P * j : 2 * P * (j + 1), :].rearrange("(p e) c -> p e c", e=2)
+            )
+            return pair
+
+        x_sb = [load_pair(x_rows, n, "x") for n in range(2)]
+        sk_sb = [load_pair(sum_k_rows, n, "sk") for n in range(4)]
+        wr_sb = [load_wr(j) for j in range(4)]
+        x_sb.extend([load_pair(x_rows, n, "x") for n in range(2, 4)])
+        wkv_sb = [load_pair(wkv_rows, n, "wkv") for n in range(2)]
+        wo_sb = [load_pair(Wo, n, "wo") for n in range(4)]
+        wkv_sb.extend([load_pair(wkv_rows, n, "wkv") for n in range(2, 4)])
+
+        x_codes = keep.tile([P, 2, PASSES, HALF], U32, name="x_codes", align_bytes=64)
+        x_scales = keep.tile([P, 2, PASSES, HALF], U8, name="x_scales", align_bytes=64)
+        wr_codes = keep.tile([P, 4, PASSES, 2 * P], U32, name="wr_codes", align_bytes=64)
+        wr_scales = keep.tile([P, 4, PASSES, 2 * P], U8, name="wr_scales", align_bytes=64)
+        wo_codes = keep.tile([P, PASSES, CH], U32, name="wo_codes", align_bytes=64)
+        wo_scales = keep.tile([P, PASSES, CH], U8, name="wo_scales", align_bytes=64)
+        g_codes = keep.tile([P, N_TILES, PASSES, P], U32, name="g_codes", align_bytes=64)
+        g_scales = keep.tile([P, N_TILES, PASSES, P], U8, name="g_scales", align_bytes=64)
+
+        def quantise(grouped, codes, scales):
+            nc.vector.quantize_mx(out=codes.bitcast(FP8X4), scales=scales, in_=grouped)
+
+        prev = keep.tile([P, 2 * BLOCKS, 2, PAD + SEQ], F32, name="prev")
+        nc.vector.memset(prev[:, :, :, 0:PAD], 0.0)
+
+        def mix_half(half):
+            planes = work.tile([P, 2 * BLOCKS, HALF], BF16, name="xm_planes", tag="planes")
+            for h in range(BLOCKS):
+                bank = psum.tile([P, HALF], F32, name="x_bank", tag="bank")
+                for k in range(4):
+                    i = 4 * half + k
+                    words = x_sb[i // 2][:, i % 2, :].bitcast(F32)
+                    nc.tensor.transpose(
+                        bank[:, P * k : P * (k + 1)], words[:, P * h : P * (h + 1)], ident[:]
+                    )
+                pairs = bank[:].bitcast(BF16).rearrange("p (s k e) -> p s k e", s=2, e=2)
+                for e in range(2):
+                    col = 2 * h + e
+                    nc.scalar.activation(
+                        out=prev[:, col, :, PAD : PAD + SEQ],
+                        in_=pairs[:, :, :, e],
+                        func=ACT.Copy,
+                        scale=rest_col[:, col : col + 1],
+                    )
+                for e in range(2):
+                    col = 2 * h + e
+                    nc.vector.scalar_tensor_tensor(
+                        out=planes[:, col, :].rearrange("p (s k) -> p s k", s=2),
+                        in0=pairs[:, :, :, e],
+                        scalar=tm_col[:, col : col + 1],
+                        in1=prev[:, col, :, PAD - 1 : PAD - 1 + SEQ],
+                        op0=ALU.mult,
+                        op1=ALU.add,
+                    )
+            groups = []
+            for c in range(PASSES):
+                grouped = work.tile([P, 4 * HALF], BF16, name="x_grouped", tag="grouped", align_bytes=64)
+                nc.vector.tensor_copy(
+                    out=grouped[:].rearrange("p (n i t) -> p n t i", i=4, t=4),
+                    in_=planes[:, 4 * c : 4 * (c + 1), :].rearrange("p t (n i) -> p n t i", i=4),
+                )
+                groups.append(grouped)
+            for c in range(PASSES):
+                quantise(groups[c][:], x_codes[:, half, c, :], x_scales[:, half, c, :])
+
+        def weight_bank(pair, c, grouped_words):
+            bank = psum.tile([P, 2, 2 * P], F32, name="w_bank", tag="bank")
+            for u in range(2):
+                h = 2 * c + u
+                for m in range(2):
+                    words = pair[:, m, :].bitcast(F32)
+                    nc.tensor.transpose(
+                        bank[:, u, P * m : P * (m + 1)], words[:, P * h : P * (h + 1)], ident[:]
+                    )
+            nc.vector.tensor_copy(out=grouped_words, in_=bank[:].rearrange("p u n -> p n u"))
+
+        def quantise_wr(j):
+            grouped = work.tile([P, 4 * HALF], BF16, name="wr_grouped", tag="grouped", align_bytes=64)
+            words = grouped[:].bitcast(F32).rearrange("p (c n u) -> p c n u", c=PASSES, u=2)
+            for c in range(PASSES):
+                weight_bank(wr_sb[j], c, words[:, c, :, :])
+            quantise(
+                grouped[:],
+                wr_codes[:, j, :, :].rearrange("p c n -> p (c n)"),
+                wr_scales[:, j, :, :].rearrange("p c n -> p (c n)"),
+            )
+
+        def quantise_wo(half, c):
+            grouped = work.tile([P, 4 * HALF], BF16, name="wo_grouped", tag="grouped", align_bytes=64)
+            words = grouped[:].bitcast(F32).rearrange("p (m n u) -> p m n u", m=2, u=2)
+            for m in range(2):
+                weight_bank(wo_sb[2 * half + m], c, words[:, m, :, :])
+            cols = slice(HALF * half, HALF * (half + 1))
+            quantise(grouped[:], wo_codes[:, c, cols], wo_scales[:, c, cols])
+
+        root = []
+        ratio = []
+
+        def reciprocal_root(i):
+            r = keep.tile([P, CH], F32, name="root" + str(i))
+            nc.scalar.activation(out=r[:], in_=sk_sb[i // 2][:, i % 2, :], func=ACT.Abs_reciprocal_sqrt)
+            root.append(r)
+
+        def divide(i):
+            nc.scalar.activation(out=root[i][:], in_=root[i][:], func=ACT.Square)
+            q = inputs.tile([P, BLOCKS, 2, P], F32, name="ratio" + str(i), tag=("sk" if i < 4 else "x"))
+            nc.gpsimd.tensor_tensor(
+                out=q[:],
+                in0=wkv_sb[i // 2][:, i % 2, :].rearrange("p (h k e) -> p h e k", h=BLOCKS, e=2),
+                in1=root[i][:].rearrange("p (h k e) -> p h e k", h=BLOCKS, e=2),
+                op=ALU.mult,
+            )
+            ratio.append(q)
+
+        gates = []
+
+        def receptance(s):
+            sig = work.tile([P, 2 * BLOCKS, SEQ], F32, name="sig", tag="planes")
+            cols = slice(SEQ * (s % 2), SEQ * (s % 2 + 1))
+            for j in range(BLOCKS):
+                acc = psum.tile([P, 2, SEQ], F32, name="r_acc", tag="bank")
+                for e in range(2):
+                    for c in range(PASSES):
+                        nc.tensor.matmul_mx(
+                            out=acc[:, e, :],
+                            lhsT=wr_codes[:, j, c, P * e : P * (e + 1)].bitcast(FP8X4),
+                            lhsT_scale=wr_scales[:, j, c, P * e : P * (e + 1)],
+                            rhs=x_codes[:, s // 2, c, cols].bitcast(FP8X4),
+                            rhs_scale=x_scales[:, s // 2, c, cols],
+                            start=(c == 0),
+                            stop=(c == PASSES - 1),
+                        )
+                nc.scalar.activation(out=sig[:, 2 * j : 2 * j + 2, :], in_=acc[:], func=ACT.Sigmoid)
+            gates.append(sig)
+
+        ratio_banks = []
+
+        def transpose_ratio(i):
+            banks = []
+            for c2 in range(PASSES):
+                bank = psum.tile([P, 4, P], F32, name="q_bank", tag="bank")
+                for t in range(4):
+                    nc.tensor.transpose(bank[:, t, :], ratio[i][:, 2 * c2 + t // 2, t % 2, :], ident[:])
+                banks.append(bank)
+            ratio_banks.append(banks)
+
+        def gate(i):
+            grouped = work.tile([P, PASSES, P, 4], BF16, name="g_grouped", tag="g_grouped", align_bytes=64)
+            cols = slice(P * (i % 2), P * (i % 2 + 1))
+            for c2 in range(PASSES):
+                nc.vector.tensor_tensor(
+                    out=grouped[:, c2, :, :],
+                    in0=gates[i // 2][:, 4 * c2 : 4 * (c2 + 1), cols].rearrange("p t k -> p k t"),
+                    in1=ratio_banks[i][c2][:].rearrange("p t k -> p k t"),
+                    op=ALU.mult,
+                )
+            quantise(
+                grouped[:].rearrange("p c k t -> p (c k t)"),
+                g_codes[:, i, :, :].rearrange("p c k -> p (c k)"),
+                g_scales[:, i, :, :].rearrange("p c k -> p (c k)"),
+            )
+
+        def project(i):
+            result = inputs.tile([P, CH], F32, name="result", tag="wr")
+            for half in range(2):
+                cols = slice(HALF * half, HALF * (half + 1))
+                acc = psum.tile([P, HALF], F32, name="o_acc", tag="bank")
+                for c2 in range(PASSES):
+                    nc.tensor.matmul_mx(
+                        out=acc[:],
+                        lhsT=g_codes[:, i, c2, :].bitcast(FP8X4),
+                        lhsT_scale=g_scales[:, i, c2, :],
+                        rhs=wo_codes[:, c2, cols].bitcast(FP8X4),
+                        rhs_scale=wo_scales[:, c2, cols],
+                        start=(c2 == 0),
+                        stop=(c2 == PASSES - 1),
+                    )
+                nc.scalar.copy(out=result[:, cols], in_=acc[:])
+            nc.sync.dma_start(out=out_rows[P * i : P * (i + 1), :], in_=result[:])
+
+        mix_half(0)
+        for j in range(4):
+            quantise_wr(j)
+        for i in range(N_TILES):
+            reciprocal_root(i)
+        mix_half(1)
+        divide(0)
+        divide(1)
+        receptance(0)
+        receptance(1)
+        divide(2)
+        divide(3)
+        quantise_wo(0, 0)
+        quantise_wo(0, 1)
+        receptance(2)
+        quantise_wo(1, 0)
+        quantise_wo(1, 1)
+        transpose_ratio(0)
+        receptance(3)
+        transpose_ratio(1)
+        divide(4)
+        divide(5)
+        for i in range(N_TILES):
+            gate(i)
+            project(i)
+            if i + 2 < N_TILES:
+                transpose_ratio(i + 2)
+            if i + 6 < N_TILES:
+                divide(i + 6)

@@ -165,7 +165,7 @@ def tile_rwkv2timemix_pa_kernel(tc, x, time_mix, Wr, wkv, sum_k, Wo, out):
         def divide(i):
             nc.scalar.activation(out=root[i][:], in_=root[i][:], func=ACT.Square)
             q = inputs.tile([P, BLOCKS, 2, P], F32, name="ratio" + str(i), tag=("sk" if i < 4 else "x"))
-            nc.gpsimd.tensor_tensor(
+            nc.vector.tensor_tensor(
                 out=q[:],
                 in0=wkv_sb[i // 2][:, i % 2, :].rearrange("p (h k e) -> p h e k", h=BLOCKS, e=2),
                 in1=root[i][:].rearrange("p (h k e) -> p h e k", h=BLOCKS, e=2),

@@ -46,6 +46,9 @@ def tile_rwkv2timemix_pa_kernel(tc, x, time_mix, Wr, wkv, sum_k, Wo, out):
         nc.vector.tensor_scalar(
             out=rest_col[:], in0=tm_col[:], scalar1=-1.0, scalar2=1.0, op0=ALU.mult, op1=ALU.add
         )
+        tm_diag = consts.tile([P, 2 * BLOCKS, P], BF16, name="tm_diag")
+        for col in range(2 * BLOCKS):
+            nc.vector.tensor_scalar_mul(out=tm_diag[:, col, :], in0=ident[:], scalar1=tm_col[:, col : col + 1])
 
         def load_pair(rows, n, name):
             pair = inputs.tile([P, 2, CH], BF16, name=name + str(n), tag=name)
@@ -62,12 +65,15 @@ def tile_rwkv2timemix_pa_kernel(tc, x, time_mix, Wr, wkv, sum_k, Wo, out):
             return pair
 
         x_sb = [load_pair(x_rows, n, "x") for n in range(2)]
-        sk_sb = [load_pair(sum_k_rows, n, "sk") for n in range(4)]
-        wr_sb = [load_wr(j) for j in range(4)]
+        sk_sb = [load_pair(sum_k_rows, n, "sk") for n in range(2)]
+        wr_sb = [load_wr(j) for j in range(2)]
+        wkv_sb = [load_pair(wkv_rows, 0, "wkv")]
+        wr_sb.extend([load_wr(j) for j in range(2, 4)])
+        wkv_sb.append(load_pair(wkv_rows, 1, "wkv"))
         x_sb.extend([load_pair(x_rows, n, "x") for n in range(2, 4)])
-        wkv_sb = [load_pair(wkv_rows, n, "wkv") for n in range(2)]
-        wo_sb = [load_pair(Wo, n, "wo") for n in range(4)]
+        sk_sb.extend([load_pair(sum_k_rows, n, "sk") for n in range(2, 4)])
         wkv_sb.extend([load_pair(wkv_rows, n, "wkv") for n in range(2, 4)])
+        wo_sb = [load_pair(Wo, n, "wo") for n in range(4)]
 
         x_codes = keep.tile([P, 2, PASSES, HALF], U32, name="x_codes", align_bytes=64)
         x_scales = keep.tile([P, 2, PASSES, HALF], U8, name="x_scales", align_bytes=64)
@@ -81,38 +87,47 @@ def tile_rwkv2timemix_pa_kernel(tc, x, time_mix, Wr, wkv, sum_k, Wo, out):
         def quantise(grouped, codes, scales):
             nc.vector.quantize_mx(out=codes.bitcast(FP8X4), scales=scales, in_=grouped)
 
-        prev = keep.tile([P, 2 * BLOCKS, 2, PAD + SEQ], F32, name="prev")
-        nc.vector.memset(prev[:, :, :, 0:PAD], 0.0)
+        xt = keep.tile([P, BLOCKS, 2, PAD + SEQ], F32, name="xt")
+        xt_pairs = xt[:].bitcast(BF16).rearrange("p h s (k e) -> p h s k e", e=2)
+        nc.vector.memset(xt_pairs[:, :, :, 0:PAD, :], 0.0)
+
+        def transpose_x(half, h):
+            bank = psum.tile([P, 2, SEQ], F32, name="x_bank", tag="bank")
+            for k in range(4):
+                i = 4 * half + k
+                words = x_sb[i // 2][:, i % 2, :].bitcast(F32)
+                nc.tensor.transpose(
+                    bank[:, k // 2, P * (k % 2) : P * (k % 2 + 1)], words[:, P * h : P * (h + 1)], ident[:]
+                )
+            nc.scalar.copy(out=xt[:, h, :, PAD : PAD + SEQ], in_=bank[:])
+
+        def mix_block(planes, h):
+            for e in range(2):
+                col = 2 * h + e
+                scaled = psum.tile([P, 2, SEQ], F32, name="x_scaled", tag="bank")
+                nc.tensor.matmul(
+                    out=scaled[:],
+                    lhsT=tm_diag[:, col, :],
+                    rhs=xt_pairs[:, h, :, PAD : PAD + SEQ, e],
+                    start=True,
+                    stop=True,
+                )
+                nc.vector.scalar_tensor_tensor(
+                    out=planes[:, col, :].rearrange("p (s k) -> p s k", s=2),
+                    in0=xt_pairs[:, h, :, PAD - 1 : PAD - 1 + SEQ, e],
+                    scalar=rest_col[:, col : col + 1],
+                    in1=scaled[:],
+                    op0=ALU.mult,
+                    op1=ALU.add,
+                )
 
         def mix_half(half):
             planes = work.tile([P, 2 * BLOCKS, HALF], BF16, name="xm_planes", tag="planes")
-            for h in range(BLOCKS):
-                bank = psum.tile([P, HALF], F32, name="x_bank", tag="bank")
-                for k in range(4):
-                    i = 4 * half + k
-                    words = x_sb[i // 2][:, i % 2, :].bitcast(F32)
-                    nc.tensor.transpose(
-                        bank[:, P * k : P * (k + 1)], words[:, P * h : P * (h + 1)], ident[:]
-                    )
-                pairs = bank[:].bitcast(BF16).rearrange("p (s k e) -> p s k e", s=2, e=2)
-                for e in range(2):
-                    col = 2 * h + e
-                    nc.scalar.activation(
-                        out=prev[:, col, :, PAD : PAD + SEQ],
-                        in_=pairs[:, :, :, e],
-                        func=ACT.Copy,
-                        scale=rest_col[:, col : col + 1],
-                    )
-                for e in range(2):
-                    col = 2 * h + e
-                    nc.vector.scalar_tensor_tensor(
-                        out=planes[:, col, :].rearrange("p (s k) -> p s k", s=2),
-                        in0=pairs[:, :, :, e],
-                        scalar=tm_col[:, col : col + 1],
-                        in1=prev[:, col, :, PAD - 1 : PAD - 1 + SEQ],
-                        op0=ALU.mult,
-                        op1=ALU.add,
-                    )
+            for h in range(BLOCKS + 1):
+                if h < BLOCKS:
+                    transpose_x(half, h)
+                if h >= 1:
+                    mix_block(planes, h - 1)
             groups = []
             for c in range(PASSES):
                 grouped = work.tile([P, 4 * HALF], BF16, name="x_grouped", tag="grouped", align_bytes=64)
@@ -124,7 +139,7 @@ def tile_rwkv2timemix_pa_kernel(tc, x, time_mix, Wr, wkv, sum_k, Wo, out):
             for c in range(PASSES):
                 quantise(groups[c][:], x_codes[:, half, c, :], x_scales[:, half, c, :])
 
-        def weight_bank(pair, c, grouped_words):
+        def weight_bank(pair, c, grouped_words, copy):
             bank = psum.tile([P, 2, 2 * P], F32, name="w_bank", tag="bank")
             for u in range(2):
                 h = 2 * c + u
@@ -133,13 +148,16 @@ def tile_rwkv2timemix_pa_kernel(tc, x, time_mix, Wr, wkv, sum_k, Wo, out):
                     nc.tensor.transpose(
                         bank[:, u, P * m : P * (m + 1)], words[:, P * h : P * (h + 1)], ident[:]
                     )
-            nc.vector.tensor_copy(out=grouped_words, in_=bank[:].rearrange("p u n -> p n u"))
+            copy(out=grouped_words, in_=bank[:].rearrange("p u n -> p n u"))
 
-        def quantise_wr(j):
+        def group_wr(j):
             grouped = work.tile([P, 4 * HALF], BF16, name="wr_grouped", tag="grouped", align_bytes=64)
             words = grouped[:].bitcast(F32).rearrange("p (c n u) -> p c n u", c=PASSES, u=2)
             for c in range(PASSES):
-                weight_bank(wr_sb[j], c, words[:, c, :, :])
+                weight_bank(wr_sb[j], c, words[:, c, :, :], nc.vector.tensor_copy)
+            return grouped
+
+        def quantise_wr(j, grouped):
             quantise(
                 grouped[:],
                 wr_codes[:, j, :, :].rearrange("p c n -> p (c n)"),
@@ -150,7 +168,7 @@ def tile_rwkv2timemix_pa_kernel(tc, x, time_mix, Wr, wkv, sum_k, Wo, out):
             grouped = work.tile([P, 4 * HALF], BF16, name="wo_grouped", tag="grouped", align_bytes=64)
             words = grouped[:].bitcast(F32).rearrange("p (m n u) -> p m n u", m=2, u=2)
             for m in range(2):
-                weight_bank(wo_sb[2 * half + m], c, words[:, m, :, :])
+                weight_bank(wo_sb[2 * half + m], c, words[:, m, :, :], nc.scalar.copy)
             cols = slice(HALF * half, HALF * (half + 1))
             quantise(grouped[:], wo_codes[:, c, cols], wo_scales[:, c, cols])
 
@@ -162,10 +180,12 @@ def tile_rwkv2timemix_pa_kernel(tc, x, time_mix, Wr, wkv, sum_k, Wo, out):
             nc.scalar.activation(out=r[:], in_=sk_sb[i // 2][:, i % 2, :], func=ACT.Abs_reciprocal_sqrt)
             root.append(r)
 
-        def divide(i):
+        def square(i):
             nc.scalar.activation(out=root[i][:], in_=root[i][:], func=ACT.Square)
-            q = inputs.tile([P, BLOCKS, 2, P], F32, name="ratio" + str(i), tag=("sk" if i < 4 else "x"))
-            nc.vector.tensor_tensor(
+
+        def divide(i, engine):
+            q = inputs.tile([P, BLOCKS, 2, P], F32, name="ratio" + str(i), tag=("x" if i % 4 < 2 else "sk"))
+            engine.tensor_tensor(
                 out=q[:],
                 in0=wkv_sb[i // 2][:, i % 2, :].rearrange("p (h k e) -> p h e k", h=BLOCKS, e=2),
                 in1=root[i][:].rearrange("p (h k e) -> p h e k", h=BLOCKS, e=2),
@@ -205,6 +225,8 @@ def tile_rwkv2timemix_pa_kernel(tc, x, time_mix, Wr, wkv, sum_k, Wo, out):
                 banks.append(bank)
             ratio_banks.append(banks)
 
+        g_grouped = []
+
         def gate(i):
             grouped = work.tile([P, PASSES, P, 4], BF16, name="g_grouped", tag="g_grouped", align_bytes=64)
             cols = slice(P * (i % 2), P * (i % 2 + 1))
@@ -215,8 +237,11 @@ def tile_rwkv2timemix_pa_kernel(tc, x, time_mix, Wr, wkv, sum_k, Wo, out):
                     in1=ratio_banks[i][c2][:].rearrange("p t k -> p k t"),
                     op=ALU.mult,
                 )
+            g_grouped.append(grouped)
+
+        def quantise_g(i):
             quantise(
-                grouped[:].rearrange("p c k t -> p (c k t)"),
+                g_grouped[i][:].rearrange("p c k t -> p (c k t)"),
                 g_codes[:, i, :, :].rearrange("p c k -> p (c k)"),
                 g_scales[:, i, :, :].rearrange("p c k -> p (c k)"),
             )
@@ -240,31 +265,48 @@ def tile_rwkv2timemix_pa_kernel(tc, x, time_mix, Wr, wkv, sum_k, Wo, out):
             nc.sync.dma_start(out=out_rows[P * i : P * (i + 1), :], in_=result[:])
 
         mix_half(0)
-        for j in range(4):
-            quantise_wr(j)
-        for i in range(N_TILES):
-            reciprocal_root(i)
+        wr_grouped = []
+        for j in range(4 + 1):
+            if j < 4:
+                wr_grouped.append(group_wr(j))
+            if j >= 1:
+                quantise_wr(j - 1, wr_grouped[j - 1])
+        for n in range(2):
+            reciprocal_root(2 * n)
+            reciprocal_root(2 * n + 1)
+            for i in (2 * n, 2 * n + 1):
+                square(i)
+                divide(i, nc.gpsimd)
         mix_half(1)
-        divide(0)
-        divide(1)
+        for i in range(4, N_TILES):
+            reciprocal_root(i)
         receptance(0)
         receptance(1)
-        divide(2)
-        divide(3)
-        quantise_wo(0, 0)
-        quantise_wo(0, 1)
-        receptance(2)
-        quantise_wo(1, 0)
-        quantise_wo(1, 1)
-        transpose_ratio(0)
-        receptance(3)
-        transpose_ratio(1)
-        divide(4)
-        divide(5)
-        for i in range(N_TILES):
+        for i in range(4, N_TILES):
+            square(i)
+        for i in range(4):
+            transpose_ratio(i)
             gate(i)
+            if i >= 1:
+                quantise_g(i - 1)
+        quantise_g(3)
+        for i in range(4, N_TILES):
+            divide(i, nc.vector)
+        for half in range(2):
+            for c in range(PASSES):
+                quantise_wo(half, c)
+        receptance(2)
+        receptance(3)
+        transpose_ratio(4)
+        transpose_ratio(5)
+        for i in range(4):
             project(i)
-            if i + 2 < N_TILES:
-                transpose_ratio(i + 2)
-            if i + 6 < N_TILES:
-                divide(i + 6)
+        transpose_ratio(6)
+        transpose_ratio(7)
+        for i in range(4, N_TILES):
+            gate(i)
+            if i >= 5:
+                quantise_g(i - 1)
+                project(i - 1)
+        quantise_g(N_TILES - 1)
+        project(N_TILES - 1)

@@ -34,6 +34,10 @@ def tile_rwkv2timemix_pa_kernel(tc, x, time_mix, Wr, wkv, sum_k, Wo, out):
     ) as inputs, tc.tile_pool(name="keep", bufs=1) as keep, tc.tile_pool(
         name="work", bufs=4
     ) as work, tc.psum_pool(name="psum", bufs=8) as psum, tc.manual_schedule():
+        ones = consts.tile([P, 1], F32, name="ones")
+        nc.vector.memset(ones[:], 1.0)
+        warm = consts.tile([P, 1], F32, name="warm")
+        nc.scalar.activation(out=warm[:], in_=ones[:], func=ACT.Abs_reciprocal_sqrt)
         ident = consts.tile([P, P], F32, name="ident")
         make_identity(nc, ident[:])
         tm_pairs = consts.tile([P, BLOCKS, 2], BF16, name="tm_pairs")
@@ -64,13 +68,25 @@ def tile_rwkv2timemix_pa_kernel(tc, x, time_mix, Wr, wkv, sum_k, Wo, out):
             )
             return pair
 
-        x_sb = [load_pair(x_rows, n, "x") for n in range(2)]
+        def load_x(half, n):
+            blocks = inputs.tile([P, 2, 4, 2 * P], BF16, name="x" + str(half) + str(n), tag="x")
+            for b in range(2):
+                h = 2 * n + b
+                nc.sync.dma_start(
+                    out=blocks[:, b, :, :],
+                    in_=x_rows[HALF * half : HALF * (half + 1), 2 * P * h : 2 * P * (h + 1)].rearrange(
+                        "(k p) c -> p k c", p=P
+                    ),
+                )
+            return blocks
+
+        x_sb = [load_x(0, n) for n in range(2)]
         sk_sb = [load_pair(sum_k_rows, n, "sk") for n in range(2)]
         wr_sb = [load_wr(j) for j in range(2)]
         wkv_sb = [load_pair(wkv_rows, 0, "wkv")]
         wr_sb.extend([load_wr(j) for j in range(2, 4)])
         wkv_sb.append(load_pair(wkv_rows, 1, "wkv"))
-        x_sb.extend([load_pair(x_rows, n, "x") for n in range(2, 4)])
+        x_sb.extend([load_x(1, n) for n in range(2)])
         sk_sb.extend([load_pair(sum_k_rows, n, "sk") for n in range(2, 4)])
         wkv_sb.extend([load_pair(wkv_rows, n, "wkv") for n in range(2, 4)])
         wo_sb = [load_pair(Wo, n, "wo") for n in range(4)]
@@ -94,11 +110,8 @@ def tile_rwkv2timemix_pa_kernel(tc, x, time_mix, Wr, wkv, sum_k, Wo, out):
         def transpose_x(half, h):
             bank = psum.tile([P, 2, SEQ], F32, name="x_bank", tag="bank")
             for k in range(4):
-                i = 4 * half + k
-                words = x_sb[i // 2][:, i % 2, :].bitcast(F32)
-                nc.tensor.transpose(
-                    bank[:, k // 2, P * (k % 2) : P * (k % 2 + 1)], words[:, P * h : P * (h + 1)], ident[:]
-                )
+                words = x_sb[2 * half + h // 2][:, h % 2, k, :].bitcast(F32)
+                nc.tensor.transpose(bank[:, k // 2, P * (k % 2) : P * (k % 2 + 1)], words, ident[:])
             nc.scalar.copy(out=xt[:, h, :, PAD : PAD + SEQ], in_=bank[:])
 
         def mix_block(planes, h):
@@ -262,7 +275,7 @@ def tile_rwkv2timemix_pa_kernel(tc, x, time_mix, Wr, wkv, sum_k, Wo, out):
                         stop=(c2 == PASSES - 1),
                     )
                 nc.scalar.copy(out=result[:, cols], in_=acc[:])
-            nc.sync.dma_start(out=out_rows[P * i : P * (i + 1), :], in_=result[:])
+                nc.sync.dma_start(out=out_rows[P * i : P * (i + 1), cols], in_=result[:, cols])
 
         mix_half(0)
         wr_grouped = []

@@ -289,8 +289,9 @@ def tile_rwkv2timemix_pa_kernel(tc, x, time_mix, Wr, wkv, sum_k, Wo, out):
             reciprocal_root(2 * n + 1)
             for i in (2 * n, 2 * n + 1):
                 square(i)
-                divide(i, nc.gpsimd)
         mix_half(1)
+        for i in range(4):
+            divide(i, nc.vector)
         for i in range(4, N_TILES):
             reciprocal_root(i)
         receptance(0)

import concourse.mybir as mybir
from concourse.masks import make_identity

F32 = mybir.dt.float32
BF16 = mybir.dt.bfloat16
U32 = mybir.dt.uint32
U8 = mybir.dt.uint8
FP8X4 = mybir.dt.float8_e4m3fn_x4
ACT = mybir.ActivationFunctionType
ALU = mybir.AluOpType

P = 128
TOKENS = 1024
SEQ = 256
CH = 1024
PASSES = 2
BLOCKS = 4
HALF = 512
N_TILES = TOKENS // P
PAD = 8

FLOPS = 2 * 2 * TOKENS * CH * CH


def tile_rwkv2timemix_pa_kernel(tc, x, time_mix, Wr, wkv, sum_k, Wo, out):
    nc = tc.nc
    x_rows = x.flatten_outer_dims()
    wkv_rows = wkv.flatten_outer_dims()
    sum_k_rows = sum_k.flatten_outer_dims()
    out_rows = out.flatten_outer_dims()

    with tc.tile_pool(name="consts", bufs=1) as consts, tc.tile_pool(
        name="inputs", bufs=4
    ) as inputs, tc.tile_pool(name="keep", bufs=1) as keep, tc.tile_pool(
        name="work", bufs=4
    ) as work, tc.psum_pool(name="psum", bufs=8) as psum, tc.manual_schedule():
        ones = consts.tile([P, 1], F32, name="ones")
        nc.vector.memset(ones[:], 1.0)
        warm = consts.tile([P, 1], F32, name="warm")
        nc.scalar.activation(out=warm[:], in_=ones[:], func=ACT.Abs_reciprocal_sqrt)
        ident = consts.tile([P, P], F32, name="ident")
        make_identity(nc, ident[:])
        tm_pairs = consts.tile([P, BLOCKS, 2], BF16, name="tm_pairs")
        nc.scalar.dma_start(
            out=tm_pairs[:], in_=time_mix.squeeze().rearrange("(h p e) -> p h e", p=P, e=2)
        )
        tm_col = consts.tile([P, 2 * BLOCKS], F32, name="tm_col")
        nc.vector.tensor_copy(out=tm_col[:], in_=tm_pairs[:].rearrange("p h e -> p (h e)"))
        rest_col = consts.tile([P, 2 * BLOCKS], F32, name="rest_col")
        nc.vector.tensor_scalar(
            out=rest_col[:], in0=tm_col[:], scalar1=-1.0, scalar2=1.0, op0=ALU.mult, op1=ALU.add
        )
        tm_diag = consts.tile([P, 2 * BLOCKS, P], BF16, name="tm_diag")
        for col in range(2 * BLOCKS):
            nc.vector.tensor_scalar_mul(out=tm_diag[:, col, :], in0=ident[:], scalar1=tm_col[:, col : col + 1])

        def load_pair(rows, n, name):
            pair = inputs.tile([P, 2, CH], BF16, name=name + str(n), tag=name)
            nc.sync.dma_start(
                out=pair[:], in_=rows[2 * P * n : 2 * P * (n + 1), :].rearrange("(i p) c -> p i c", p=P)
            )
            return pair

        def load_wr(j):
            pair = inputs.tile([P, 2, CH], BF16, name="wr" + str(j), tag="wr")
            nc.sync.dma_start(
                out=pair[:], in_=Wr[2 * P * j : 2 * P * (j + 1), :].rearrange("(p e) c -> p e c", e=2)
            )
            return pair

        def load_x(half, n):
            blocks = inputs.tile([P, 2, 4, 2 * P], BF16, name="x" + str(half) + str(n), tag="x")
            for b in range(2):
                h = 2 * n + b
                nc.sync.dma_start(
                    out=blocks[:, b, :, :],
                    in_=x_rows[HALF * half : HALF * (half + 1), 2 * P * h : 2 * P * (h + 1)].rearrange(
                        "(k p) c -> p k c", p=P
                    ),
                )
            return blocks

        x_sb = [load_x(0, n) for n in range(2)]
        sk_sb = [load_pair(sum_k_rows, n, "sk") for n in range(2)]
        wr_sb = [load_wr(j) for j in range(2)]
        wkv_sb = [load_pair(wkv_rows, 0, "wkv")]
        wr_sb.extend([load_wr(j) for j in range(2, 4)])
        wkv_sb.append(load_pair(wkv_rows, 1, "wkv"))
        x_sb.extend([load_x(1, n) for n in range(2)])
        sk_sb.extend([load_pair(sum_k_rows, n, "sk") for n in range(2, 4)])
        wkv_sb.extend([load_pair(wkv_rows, n, "wkv") for n in range(2, 4)])
        wo_sb = [load_pair(Wo, n, "wo") for n in range(4)]

        x_codes = keep.tile([P, 2, PASSES, HALF], U32, name="x_codes", align_bytes=64)
        x_scales = keep.tile([P, 2, PASSES, HALF], U8, name="x_scales", align_bytes=64)
        wr_codes = keep.tile([P, 4, PASSES, 2 * P], U32, name="wr_codes", align_bytes=64)
        wr_scales = keep.tile([P, 4, PASSES, 2 * P], U8, name="wr_scales", align_bytes=64)
        wo_codes = keep.tile([P, PASSES, CH], U32, name="wo_codes", align_bytes=64)
        wo_scales = keep.tile([P, PASSES, CH], U8, name="wo_scales", align_bytes=64)
        g_codes = keep.tile([P, N_TILES, PASSES, P], U32, name="g_codes", align_bytes=64)
        g_scales = keep.tile([P, N_TILES, PASSES, P], U8, name="g_scales", align_bytes=64)

        def quantise(grouped, codes, scales):
            nc.vector.quantize_mx(out=codes.bitcast(FP8X4), scales=scales, in_=grouped)

        xt = keep.tile([P, BLOCKS, 2, PAD + SEQ], F32, name="xt")
        xt_pairs = xt[:].bitcast(BF16).rearrange("p h s (k e) -> p h s k e", e=2)
        nc.vector.memset(xt_pairs[:, :, :, 0:PAD, :], 0.0)

        def transpose_x(half, h):
            bank = psum.tile([P, 2, SEQ], F32, name="x_bank", tag="bank")
            for k in range(4):
                words = x_sb[2 * half + h // 2][:, h % 2, k, :].bitcast(F32)
                nc.tensor.transpose(bank[:, k // 2, P * (k % 2) : P * (k % 2 + 1)], words, ident[:])
            nc.scalar.copy(out=xt[:, h, :, PAD : PAD + SEQ], in_=bank[:])

        def mix_block(planes, h):
            for e in range(2):
                col = 2 * h + e
                scaled = psum.tile([P, 2, SEQ], F32, name="x_scaled", tag="bank")
                nc.tensor.matmul(
                    out=scaled[:],
                    lhsT=tm_diag[:, col, :],
                    rhs=xt_pairs[:, h, :, PAD : PAD + SEQ, e],
                    start=True,
                    stop=True,
                )
                nc.vector.scalar_tensor_tensor(
                    out=planes[:, col, :].rearrange("p (s k) -> p s k", s=2),
                    in0=xt_pairs[:, h, :, PAD - 1 : PAD - 1 + SEQ, e],
                    scalar=rest_col[:, col : col + 1],
                    in1=scaled[:],
                    op0=ALU.mult,
                    op1=ALU.add,
                )

        def mix_half(half):
            planes = work.tile([P, 2 * BLOCKS, HALF], BF16, name="xm_planes", tag="planes")
            for h in range(BLOCKS + 1):
                if h < BLOCKS:
                    transpose_x(half, h)
                if h >= 1:
                    mix_block(planes, h - 1)
            groups = []
            for c in range(PASSES):
                grouped = work.tile([P, 4 * HALF], BF16, name="x_grouped", tag="grouped", align_bytes=64)
                nc.vector.tensor_copy(
                    out=grouped[:].rearrange("p (n i t) -> p n t i", i=4, t=4),
                    in_=planes[:, 4 * c : 4 * (c + 1), :].rearrange("p t (n i) -> p n t i", i=4),
                )
                groups.append(grouped)
            for c in range(PASSES):
                quantise(groups[c][:], x_codes[:, half, c, :], x_scales[:, half, c, :])

        def weight_bank(pair, c, grouped_words, copy):
            bank = psum.tile([P, 2, 2 * P], F32, name="w_bank", tag="bank")
            for u in range(2):
                h = 2 * c + u
                for m in range(2):
                    words = pair[:, m, :].bitcast(F32)
                    nc.tensor.transpose(
                        bank[:, u, P * m : P * (m + 1)], words[:, P * h : P * (h + 1)], ident[:]
                    )
            copy(out=grouped_words, in_=bank[:].rearrange("p u n -> p n u"))

        def group_wr(j):
            grouped = work.tile([P, 4 * HALF], BF16, name="wr_grouped", tag="grouped", align_bytes=64)
            words = grouped[:].bitcast(F32).rearrange("p (c n u) -> p c n u", c=PASSES, u=2)
            for c in range(PASSES):
                weight_bank(wr_sb[j], c, words[:, c, :, :], nc.vector.tensor_copy)
            return grouped

        def quantise_wr(j, grouped):
            quantise(
                grouped[:],
                wr_codes[:, j, :, :].rearrange("p c n -> p (c n)"),
                wr_scales[:, j, :, :].rearrange("p c n -> p (c n)"),
            )

        def quantise_wo(half, c):
            grouped = work.tile([P, 4 * HALF], BF16, name="wo_grouped", tag="grouped", align_bytes=64)
            words = grouped[:].bitcast(F32).rearrange("p (m n u) -> p m n u", m=2, u=2)
            for m in range(2):
                weight_bank(wo_sb[2 * half + m], c, words[:, m, :, :], nc.scalar.copy)
            cols = slice(HALF * half, HALF * (half + 1))
            quantise(grouped[:], wo_codes[:, c, cols], wo_scales[:, c, cols])

        root = []
        ratio = []

        def reciprocal_root(i):
            r = keep.tile([P, CH], F32, name="root" + str(i))
            nc.scalar.activation(out=r[:], in_=sk_sb[i // 2][:, i % 2, :], func=ACT.Abs_reciprocal_sqrt)
            root.append(r)

        def square(i):
            nc.scalar.activation(out=root[i][:], in_=root[i][:], func=ACT.Square)

        def divide(i, engine):
            q = inputs.tile([P, BLOCKS, 2, P], F32, name="ratio" + str(i), tag=("x" if i % 4 < 2 else "sk"))
            engine.tensor_tensor(
                out=q[:],
                in0=wkv_sb[i // 2][:, i % 2, :].rearrange("p (h k e) -> p h e k", h=BLOCKS, e=2),
                in1=root[i][:].rearrange("p (h k e) -> p h e k", h=BLOCKS, e=2),
                op=ALU.mult,
            )
            ratio.append(q)

        gates = []

        def receptance(s):
            sig = work.tile([P, 2 * BLOCKS, SEQ], F32, name="sig", tag="planes")
            cols = slice(SEQ * (s % 2), SEQ * (s % 2 + 1))
            for j in range(BLOCKS):
                acc = psum.tile([P, 2, SEQ], F32, name="r_acc", tag="bank")
                for e in range(2):
                    for c in range(PASSES):
                        nc.tensor.matmul_mx(
                            out=acc[:, e, :],
                            lhsT=wr_codes[:, j, c, P * e : P * (e + 1)].bitcast(FP8X4),
                            lhsT_scale=wr_scales[:, j, c, P * e : P * (e + 1)],
                            rhs=x_codes[:, s // 2, c, cols].bitcast(FP8X4),
                            rhs_scale=x_scales[:, s // 2, c, cols],
                            start=(c == 0),
                            stop=(c == PASSES - 1),
                        )
                nc.scalar.activation(out=sig[:, 2 * j : 2 * j + 2, :], in_=acc[:], func=ACT.Sigmoid)
            gates.append(sig)

        ratio_banks = []

        def transpose_ratio(i):
            banks = []
            for c2 in range(PASSES):
                bank = psum.tile([P, 4, P], F32, name="q_bank", tag="bank")
                for t in range(4):
                    nc.tensor.transpose(bank[:, t, :], ratio[i][:, 2 * c2 + t // 2, t % 2, :], ident[:])
                banks.append(bank)
            ratio_banks.append(banks)

        g_grouped = []

        def gate(i):
            grouped = work.tile([P, PASSES, P, 4], BF16, name="g_grouped", tag="g_grouped", align_bytes=64)
            cols = slice(P * (i % 2), P * (i % 2 + 1))
            for c2 in range(PASSES):
                nc.vector.tensor_tensor(
                    out=grouped[:, c2, :, :],
                    in0=gates[i // 2][:, 4 * c2 : 4 * (c2 + 1), cols].rearrange("p t k -> p k t"),
                    in1=ratio_banks[i][c2][:].rearrange("p t k -> p k t"),
                    op=ALU.mult,
                )
            g_grouped.append(grouped)

        def quantise_g(i):
            quantise(
                g_grouped[i][:].rearrange("p c k t -> p (c k t)"),
                g_codes[:, i, :, :].rearrange("p c k -> p (c k)"),
                g_scales[:, i, :, :].rearrange("p c k -> p (c k)"),
            )

        def project(i):
            result = inputs.tile([P, CH], F32, name="result", tag="wr")
            for half in range(2):
                cols = slice(HALF * half, HALF * (half + 1))
                acc = psum.tile([P, HALF], F32, name="o_acc", tag="bank")
                for c2 in range(PASSES):
                    nc.tensor.matmul_mx(
                        out=acc[:],
                        lhsT=g_codes[:, i, c2, :].bitcast(FP8X4),
                        lhsT_scale=g_scales[:, i, c2, :],
                        rhs=wo_codes[:, c2, cols].bitcast(FP8X4),
                        rhs_scale=wo_scales[:, c2, cols],
                        start=(c2 == 0),
                        stop=(c2 == PASSES - 1),
                    )
                nc.scalar.copy(out=result[:, cols], in_=acc[:])
                nc.sync.dma_start(out=out_rows[P * i : P * (i + 1), cols], in_=result[:, cols])

        mix_half(0)
        wr_grouped = []
        for j in range(4 + 1):
            if j < 4:
                wr_grouped.append(group_wr(j))
            if j >= 1:
                quantise_wr(j - 1, wr_grouped[j - 1])
        for n in range(2):
            reciprocal_root(2 * n)
            reciprocal_root(2 * n + 1)
            for i in (2 * n, 2 * n + 1):
                square(i)
        mix_half(1)
        for i in range(4):
            divide(i, nc.vector)
        for i in range(4, N_TILES):
            reciprocal_root(i)
        receptance(0)
        receptance(1)
        for i in range(4, N_TILES):
            square(i)
        for i in range(4):
            transpose_ratio(i)
            gate(i)
            if i >= 1:
                quantise_g(i - 1)
        quantise_g(3)
        for i in range(4, N_TILES):
            divide(i, nc.vector)
        for half in range(2):
            for c in range(PASSES):
                quantise_wo(half, c)
        receptance(2)
        receptance(3)
        transpose_ratio(4)
        transpose_ratio(5)
        for i in range(4):
            project(i)
        transpose_ratio(6)
        transpose_ratio(7)
        for i in range(4, N_TILES):
            gate(i)
            if i >= 5:
                quantise_g(i - 1)
                project(i - 1)
        quantise_g(N_TILES - 1)
        project(N_TILES - 1)
